import numpy as np
import ml_dtypes

BF16 = ml_dtypes.bfloat16


def bf(x):
    return np.asarray(x, np.float32).astype(BF16)


def f32(x):
    return np.asarray(x, np.float32)


def f64(x):
    return np.asarray(x).astype(np.float64)


def striped(idx):
    return np.tile(idx.reshape(-1, 16).T, (8, 1))


S, D, HD, M, N = 2048, 128, 128, 256, 256
FREQ = 10000.0
GAIN = 0.42


def abs_pos_bias():
    pos = np.arange(N, dtype=np.float64)[:, None]
    i = np.arange(N // 2, dtype=np.float64)[None, :]
    ang = pos / FREQ ** (2.0 * i / D)
    return np.stack([np.sin(ang), np.cos(ang)], axis=-1).reshape(N, N)


def setup_inputs():
    return {"table": bf(np.random.standard_normal((S, D))), "w": bf(GAIN * np.random.standard_normal((D, M)) / np.sqrt(D)), "pos_bias": f32(abs_pos_bias()), "offs": striped(np.random.permutation(S)[:N])}


def reference(table, w, pos_bias, offs):
    idx = offs[:16].T.reshape(-1)
    qk = f64(w).T @ f64(table)[idx].T
    q, k = qk[:HD], qk[HD:]
    scores = q.T @ k + f64(pos_bias)
    e = np.exp(scores - scores.max(axis=1, keepdims=True))
    return e / e.sum(axis=1, keepdims=True)

@@ -1,0 +1,79 @@
+import concourse.mybir as mybir
+from concourse.masks import make_identity
+
+S, D, HD, N = 2048, 128, 128, 256
+P = 128
+TOKEN_BLOCKS = S // P
+BLOCKS_PER_GROUP = 4
+GROUPS = TOKEN_BLOCKS // BLOCKS_PER_GROUP
+GROUP_TOKENS = BLOCKS_PER_GROUP * P
+ROW_BLOCKS = N // P
+FLOPS = 2 * D * (2 * HD) * N + 2 * HD * N * N
+
+BF16, F32, U16 = mybir.dt.bfloat16, mybir.dt.float32, mybir.dt.uint16
+ADD = mybir.AluOpType.add
+EXP = mybir.ActivationFunctionType.Exp
+ALONG_ROW = mybir.AxisListType.X
+
+
+def tile_selfattention_kernel(tc, table, w, pos_bias, offs, out):
+    nc = tc.nc
+    with (
+        tc.tile_pool(name="held", bufs=1) as held,
+        tc.tile_pool(name="work", bufs=ROW_BLOCKS) as work,
+        tc.psum_pool(name="psum_flip", bufs=GROUPS) as psum_flip,
+        tc.psum_pool(name="psum_qk", bufs=1) as psum_qk,
+        tc.psum_pool(name="psum_scores", bufs=ROW_BLOCKS) as psum_scores,
+    ):
+        offsets = held.tile([P, N // 16], U16, name="offsets")
+        nc.sync.dma_start(offsets[:], offs)
+        table_blocks = table.rearrange("(a p) d -> p a d", p=P)
+        rows = []
+        for g in range(GROUPS):
+            group_rows = held.tile([P, BLOCKS_PER_GROUP, D], BF16, name=f"rows{g}")
+            queue = nc.sync if g % 2 == 0 else nc.scalar
+            queue.dma_start(group_rows[:], table_blocks[:, g * BLOCKS_PER_GROUP : (g + 1) * BLOCKS_PER_GROUP, :])
+            rows.append(group_rows)
+        weights = held.tile([D, 2 * HD], BF16, name="weights")
+        nc.gpsimd.dma_start(weights[:], w)
+        bias = held.tile([P, ROW_BLOCKS, N], F32, name="bias")
+        nc.gpsimd.dma_start(bias[:], pos_bias.rearrange("(b p) s -> p b s", p=P))
+        identity = held.tile([P, P], BF16, name="identity")
+        make_identity(nc, identity[:])
+
+        table_t = held.tile([D, S], BF16, name="table_t")
+        for g in range(GROUPS):
+            flipped = psum_flip.tile([D, GROUP_TOKENS], BF16, name="flipped")
+            for a in range(BLOCKS_PER_GROUP):
+                nc.tensor.transpose(flipped[:, a * P : (a + 1) * P], rows[g][:, a, :], identity[:])
+            columns = table_t[:, g * GROUP_TOKENS : (g + 1) * GROUP_TOKENS]
+            if g % 2 == 0:
+                nc.vector.tensor_copy(columns, flipped[:])
+            else:
+                nc.scalar.copy(columns, flipped[:])
+
+        q_psum = psum_qk.tile([HD, N], F32, name="q_psum")
+        k_psum = psum_qk.tile([HD, N], F32, name="k_psum")
+        nc.tensor.matmul(q_psum[:], weights[:, 0:HD], table_t[:].indirect(offsets[:]))
+        nc.tensor.matmul(k_psum[:], weights[:, HD : 2 * HD], table_t[:].indirect(offsets[:]))
+        q = held.tile([HD, N], BF16, name="q")
+        k = held.tile([HD, N], BF16, name="k")
+        nc.vector.tensor_copy(q[:], q_psum[:])
+        nc.scalar.copy(k[:], k_psum[:])
+
+        for b in range(ROW_BLOCKS):
+            qk_psum = psum_scores.tile([P, N], F32, name="qk_psum")
+            nc.tensor.matmul(qk_psum[:], q[:, b * P : (b + 1) * P], k[:])
+            scores = work.tile([P, N], F32, name="scores")
+            nc.vector.tensor_tensor(scores[:], qk_psum[:], bias[:, b, :], ADD)
+
+            neg_max = work.tile([P, 1], F32, name="neg_max")
+            nc.vector.reduce_max(neg_max[:], scores[:], axis=ALONG_ROW, negate=True)
+            e = work.tile([P, N], F32, name="e")
+            row_sum = work.tile([P, 1], F32, name="row_sum")
+            nc.scalar.activation(e[:], scores[:], EXP, bias=neg_max[:], scale=1.0, accum_out=row_sum[:])
+            inv_sum = work.tile([P, 1], F32, name="inv_sum")
+            nc.vector.reciprocal(inv_sum[:], row_sum[:])
+            prob = work.tile([P, N], F32, name="prob")
+            nc.vector.tensor_scalar_mul(prob[:], e[:], inv_sum[:])
+            nc.sync.dma_start(out[b * P : (b + 1) * P, :], prob[:])

@@ -35,9 +35,9 @@ def tile_selfattention_kernel(tc, table, w, pos_bias, offs, out):
             queue.dma_start(group_rows[:], table_blocks[:, g * BLOCKS_PER_GROUP : (g + 1) * BLOCKS_PER_GROUP, :])
             rows.append(group_rows)
         weights = held.tile([D, 2 * HD], BF16, name="weights")
-        nc.gpsimd.dma_start(weights[:], w)
+        nc.sync.dma_start(weights[:], w)
         bias = held.tile([P, ROW_BLOCKS, N], F32, name="bias")
-        nc.gpsimd.dma_start(bias[:], pos_bias.rearrange("(b p) s -> p b s", p=P))
+        nc.scalar.dma_start(bias[:], pos_bias.rearrange("(b p) s -> p b s", p=P))
         identity = held.tile([P, P], BF16, name="identity")
         make_identity(nc, identity[:])
 

@@ -27,12 +27,12 @@ def tile_selfattention_kernel(tc, table, w, pos_bias, offs, out):
     ):
         offsets = held.tile([P, N // 16], U16, name="offsets")
         nc.sync.dma_start(offsets[:], offs)
-        table_blocks = table.rearrange("(a p) d -> p a d", p=P)
+        table_groups = table.rearrange("(g p j) d -> g p j d", p=P, j=BLOCKS_PER_GROUP)
         rows = []
         for g in range(GROUPS):
             group_rows = held.tile([P, BLOCKS_PER_GROUP, D], BF16, name=f"rows{g}")
             queue = nc.sync if g % 2 == 0 else nc.scalar
-            queue.dma_start(group_rows[:], table_blocks[:, g * BLOCKS_PER_GROUP : (g + 1) * BLOCKS_PER_GROUP, :])
+            queue.dma_start(group_rows[:], table_groups[g])
             rows.append(group_rows)
         weights = held.tile([D, 2 * HD], BF16, name="weights")
         nc.sync.dma_start(weights[:], w)
@@ -43,14 +43,15 @@ def tile_selfattention_kernel(tc, table, w, pos_bias, offs, out):
 
         table_t = held.tile([D, S], BF16, name="table_t")
         for g in range(GROUPS):
-            flipped = psum_flip.tile([D, GROUP_TOKENS], BF16, name="flipped")
-            for a in range(BLOCKS_PER_GROUP):
-                nc.tensor.transpose(flipped[:, a * P : (a + 1) * P], rows[g][:, a, :], identity[:])
-            columns = table_t[:, g * GROUP_TOKENS : (g + 1) * GROUP_TOKENS]
+            flipped = psum_flip.tile([D, BLOCKS_PER_GROUP, P], BF16, name="flipped")
+            for j in range(BLOCKS_PER_GROUP):
+                nc.tensor.transpose(flipped[:, j, :], rows[g][:, j, :], identity[:])
+            columns = table_t[:, g * GROUP_TOKENS : (g + 1) * GROUP_TOKENS].rearrange("d (p j) -> d p j", j=BLOCKS_PER_GROUP)
+            in_token_order = flipped[:].rearrange("d j p -> d p j")
             if g % 2 == 0:
-                nc.vector.tensor_copy(columns, flipped[:])
+                nc.vector.tensor_copy(columns, in_token_order)
             else:
-                nc.scalar.copy(columns, flipped[:])
+                nc.scalar.copy(columns, in_token_order)
 
         q_psum = psum_qk.tile([HD, N], F32, name="q_psum")
         k_psum = psum_qk.tile([HD, N], F32, name="k_psum")

import concourse.mybir as mybir
from concourse.masks import make_identity

S, D, HD, N = 2048, 128, 128, 256
P = 128
TOKEN_BLOCKS = S // P
BLOCKS_PER_GROUP = 4
GROUPS = TOKEN_BLOCKS // BLOCKS_PER_GROUP
GROUP_TOKENS = BLOCKS_PER_GROUP * P
ROW_BLOCKS = N // P
FLOPS = 2 * D * (2 * HD) * N + 2 * HD * N * N

BF16, F32, U16 = mybir.dt.bfloat16, mybir.dt.float32, mybir.dt.uint16
ADD = mybir.AluOpType.add
EXP = mybir.ActivationFunctionType.Exp
ALONG_ROW = mybir.AxisListType.X


def tile_selfattention_kernel(tc, table, w, pos_bias, offs, out):
    nc = tc.nc
    with (
        tc.tile_pool(name="held", bufs=1) as held,
        tc.tile_pool(name="work", bufs=ROW_BLOCKS) as work,
        tc.psum_pool(name="psum_flip", bufs=GROUPS) as psum_flip,
        tc.psum_pool(name="psum_qk", bufs=1) as psum_qk,
        tc.psum_pool(name="psum_scores", bufs=ROW_BLOCKS) as psum_scores,
    ):
        offsets = held.tile([P, N // 16], U16, name="offsets")
        nc.sync.dma_start(offsets[:], offs)
        table_groups = table.rearrange("(g p j) d -> g p j d", p=P, j=BLOCKS_PER_GROUP)
        rows = []
        for g in range(GROUPS):
            group_rows = held.tile([P, BLOCKS_PER_GROUP, D], BF16, name=f"rows{g}")
            queue = nc.sync if g % 2 == 0 else nc.scalar
            queue.dma_start(group_rows[:], table_groups[g])
            rows.append(group_rows)
        weights = held.tile([D, 2 * HD], BF16, name="weights")
        nc.sync.dma_start(weights[:], w)
        bias = held.tile([P, ROW_BLOCKS, N], F32, name="bias")
        nc.scalar.dma_start(bias[:], pos_bias.rearrange("(b p) s -> p b s", p=P))
        identity = held.tile([P, P], BF16, name="identity")
        make_identity(nc, identity[:])

        table_t = held.tile([D, S], BF16, name="table_t")
        for g in range(GROUPS):
            flipped = psum_flip.tile([D, BLOCKS_PER_GROUP, P], BF16, name="flipped")
            for j in range(BLOCKS_PER_GROUP):
                nc.tensor.transpose(flipped[:, j, :], rows[g][:, j, :], identity[:])
            columns = table_t[:, g * GROUP_TOKENS : (g + 1) * GROUP_TOKENS].rearrange("d (p j) -> d p j", j=BLOCKS_PER_GROUP)
            in_token_order = flipped[:].rearrange("d j p -> d p j")
            if g % 2 == 0:
                nc.vector.tensor_copy(columns, in_token_order)
            else:
                nc.scalar.copy(columns, in_token_order)

        q_psum = psum_qk.tile([HD, N], F32, name="q_psum")
        k_psum = psum_qk.tile([HD, N], F32, name="k_psum")
        nc.tensor.matmul(q_psum[:], weights[:, 0:HD], table_t[:].indirect(offsets[:]))
        nc.tensor.matmul(k_psum[:], weights[:, HD : 2 * HD], table_t[:].indirect(offsets[:]))
        q = held.tile([HD, N], BF16, name="q")
        k = held.tile([HD, N], BF16, name="k")
        nc.vector.tensor_copy(q[:], q_psum[:])
        nc.scalar.copy(k[:], k_psum[:])

        for b in range(ROW_BLOCKS):
            qk_psum = psum_scores.tile([P, N], F32, name="qk_psum")
            nc.tensor.matmul(qk_psum[:], q[:, b * P : (b + 1) * P], k[:])
            scores = work.tile([P, N], F32, name="scores")
            nc.vector.tensor_tensor(scores[:], qk_psum[:], bias[:, b, :], ADD)

            neg_max = work.tile([P, 1], F32, name="neg_max")
            nc.vector.reduce_max(neg_max[:], scores[:], axis=ALONG_ROW, negate=True)
            e = work.tile([P, N], F32, name="e")
            row_sum = work.tile([P, 1], F32, name="row_sum")
            nc.scalar.activation(e[:], scores[:], EXP, bias=neg_max[:], scale=1.0, accum_out=row_sum[:])
            inv_sum = work.tile([P, 1], F32, name="inv_sum")
            nc.vector.reciprocal(inv_sum[:], row_sum[:])
            prob = work.tile([P, N], F32, name="prob")
            nc.vector.tensor_scalar_mul(prob[:], e[:], inv_sum[:])
            nc.sync.dma_start(out[b * P : (b + 1) * P, :], prob[:])
